import numpy as np
import ml_dtypes


def mxq(x, axis, fmt="e4m3"):
    dtype, down = {"e4m3": (ml_dtypes.float8_e4m3fn, 7), "e5m2": (ml_dtypes.float8_e5m2, 14)}[fmt]
    v = np.moveaxis(np.asarray(x, np.float32).astype(ml_dtypes.bfloat16).astype(np.float64), axis, -1)
    blocks = v.reshape(v.shape[:-1] + (-1, 32))
    amax = np.abs(blocks).max(-1, keepdims=True)
    byte = np.maximum(np.where(amax > 0, np.frexp(amax)[1] - 1 + 127, 0) - down, 1)
    scale = np.exp2(byte - 127.0)
    codes = (blocks / scale).astype(np.float32).astype(dtype).astype(np.float64)
    return np.moveaxis((codes * scale).reshape(v.shape), -1, axis)


WIDE = False


def mx_kscale(k):
    if not WIDE:
        return np.ones(k)
    levels = np.array([10, -10, 5, -5, 0])
    a = np.random.permutation(np.resize(levels, k // 512 * 4)).reshape(k // 512, 4)
    idx = np.arange(k)
    return np.exp2(a[idx // 512, idx % 128 // 32])


BF16 = ml_dtypes.bfloat16


def bf(x):
    return np.asarray(x, np.float32).astype(BF16)


def f64(x):
    return np.asarray(x).astype(np.float64)


E, T, H, F = 1, 256, 8192, 512


def gelu_tanh(v):
    return 0.5 * v * (1.0 + np.tanh(np.sqrt(2.0 / np.pi) * (v + 0.044715 * v**3)))


def setup_inputs():
    s, t = mx_kscale(H), mx_kscale(F)
    w1 = np.random.standard_normal((E, H, 2 * F)) / np.sqrt(H) / s[:, None]
    w1[:, :, F:] *= t
    w2 = np.random.standard_normal((E, F, H)) * 1.5 / np.sqrt(F) / t[:, None]
    return {"x": bf(np.random.standard_normal((E, T, H)) * s),
            "weight1": bf(w1.reshape(H, E * 2 * F)),
            "weight2": bf(w2.reshape(E * F, H))}


def reference(x, weight1, weight2):
    w1 = f64(weight1).reshape(E, H, 2 * F)
    w2 = f64(weight2).reshape(E, F, H)
    h = mxq(f64(x), 2, "e4m3") @ mxq(w1, 1, "e4m3")
    a, b = h[..., :F], h[..., F:]
    g = gelu_tanh(a) * b
    return mxq(g, 2, "e4m3") @ mxq(w2, 1, "e4m3")

@@ -1,0 +1,243 @@
+from contextlib import ExitStack
+
+import concourse.mybir as mybir
+from concourse.masks import make_identity
+
+BF16 = mybir.dt.bfloat16
+F32 = mybir.dt.float32
+U32 = mybir.dt.uint32
+U8 = mybir.dt.uint8
+FP8X4 = mybir.dt.float8_e4m3fn_x4
+
+P = 128
+PACK = 4
+K_PASS = P * PACK
+
+T = 256
+H = 8192
+F = 512
+T_TILES = T // P
+F_TILES = F // P
+
+FLOPS = 2 * T * H * (2 * F) + 2 * T * F * H
+
+X_CHUNK_PASSES = 4
+X_CHUNKS = H // (K_PASS * X_CHUNK_PASSES)
+X_CHUNK_COLS = K_PASS * X_CHUNK_PASSES
+WORD_PAIRS = 2
+
+UNIT_COLS = 1024
+W1_UNITS = H // K_PASS
+W2_UNITS = H // UNIT_COLS
+UNITS = W1_UNITS + W2_UNITS
+CHUNK_UNITS = 2
+W1_CHUNKS = W1_UNITS // CHUNK_UNITS
+CHUNKS = UNITS // CHUNK_UNITS
+RAW_BUFS = 5
+
+RUN = 4
+W1_SCALAR_COLS = 512
+W2_SCALAR_COLS = 128
+
+N_MOVE = 512
+
+
+def tile_expert_k_kernel(tc, x, weight1, weight2, out):
+    nc = tc.nc
+
+    x_rows = x.rearrange("e (tt p) h -> p (e tt) h", p=P)
+    out_rows = out.rearrange("e (tt p) h -> p (e tt) h", p=P)
+    w1_chunks = weight1.rearrange("(c u p j) n -> c p u (j n)", u=CHUNK_UNITS, p=P, j=PACK)
+    w2_rows = weight2.rearrange("(j p) n -> p j n", p=P)
+
+    with ExitStack() as ctx:
+        consts = ctx.enter_context(tc.tile_pool(name="consts", bufs=1))
+        x_raw_pool = ctx.enter_context(tc.tile_pool(name="x_raw", bufs=X_CHUNKS))
+        x_grouped_pool = ctx.enter_context(tc.tile_pool(name="x_grouped", bufs=2))
+        raw_pool = ctx.enter_context(tc.tile_pool(name="raw", bufs=RAW_BUFS))
+        grouped_pool = ctx.enter_context(tc.tile_pool(name="grouped", bufs=3))
+        mx_pool = ctx.enter_context(tc.tile_pool(name="mx", bufs=4))
+        out_pool = ctx.enter_context(tc.tile_pool(name="out", bufs=3))
+        psum = ctx.enter_context(tc.psum_pool(name="psum", bufs=8))
+
+        x_raw = []
+        for c in range(X_CHUNKS):
+            x_chunk = x_raw_pool.tile([P, T_TILES, X_CHUNK_COLS], BF16)
+            cols = slice(c * X_CHUNK_COLS, (c + 1) * X_CHUNK_COLS)
+            nc.sync.dma_start(out=x_chunk[:], in_=x_rows[:, :, cols])
+            x_raw.append(x_chunk)
+
+        unit_rows = []
+
+        def load_chunk(chunk):
+            if chunk < W1_CHUNKS:
+                raw1 = raw_pool.tile([P, CHUNK_UNITS, PACK, UNIT_COLS], BF16, tag="raw")
+                nc.sync.dma_start(
+                    out=raw1[:].rearrange("p u j n -> p u (j n)"), in_=w1_chunks[chunk]
+                )
+                for u in range(CHUNK_UNITS):
+                    unit_rows.append(raw1[:, u])
+            else:
+                raw2 = raw_pool.tile([P, PACK, CHUNK_UNITS * UNIT_COLS], BF16, tag="raw")
+                first = (chunk - W1_CHUNKS) * CHUNK_UNITS * UNIT_COLS
+                nc.sync.dma_start(
+                    out=raw2[:], in_=w2_rows[:, :, first : first + CHUNK_UNITS * UNIT_COLS]
+                )
+                for u in range(CHUNK_UNITS):
+                    unit_rows.append(raw2[:, :, u * UNIT_COLS : (u + 1) * UNIT_COLS])
+
+        for chunk in range(RAW_BUFS):
+            load_chunk(chunk)
+
+        identity = consts.tile([P, P], F32)
+        make_identity(nc, identity[:])
+        warm = consts.tile([P, 2], F32)
+        nc.vector.memset(warm[:], 0.0)
+        nc.scalar.activation(
+            out=warm[:, 1:2], in_=warm[:, 0:1], func=mybir.ActivationFunctionType.Gelu_apprx_tanh
+        )
+
+        x_codes = consts.tile([P, W1_UNITS * T], U32, align_bytes=64)
+        x_scales = consts.tile([P, W1_UNITS * T], U8, align_bytes=64)
+
+        def transpose_x_chunk(c):
+            x_grouped = x_grouped_pool.tile([P, X_CHUNK_PASSES, T, PACK], BF16, align_bytes=64)
+            grouped_words = x_grouped[:].bitcast(F32)
+            x_words = x_raw[c][:].bitcast(F32).rearrange(
+                "p tt (s m w) -> p tt s w m", m=P, w=WORD_PAIRS
+            )
+            for s in range(X_CHUNK_PASSES):
+                bank = psum.tile([P, WORD_PAIRS, T], F32, tag="bank")
+                for w in range(WORD_PAIRS):
+                    for tt in range(T_TILES):
+                        nc.tensor.transpose(
+                            bank[:, w, tt * P : (tt + 1) * P], x_words[:, tt, s, w, :], identity[:]
+                        )
+                pairs = bank[:].rearrange("p w t -> p t w")
+                if s % 2 == 0:
+                    nc.scalar.copy(out=grouped_words[:, s], in_=pairs)
+                else:
+                    nc.vector.tensor_copy(out=grouped_words[:, s], in_=pairs)
+            return x_grouped
+
+        def quantise_x_chunk(c, x_grouped):
+            cols = slice(c * X_CHUNK_PASSES * T, (c + 1) * X_CHUNK_PASSES * T)
+            nc.vector.quantize_mx(
+                out=x_codes[:, cols].bitcast(FP8X4),
+                scales=x_scales[:, cols],
+                in_=x_grouped[:].rearrange("p s t j -> p (s t j)"),
+            )
+
+        x_grouped_tiles = []
+        for c in range(X_CHUNKS + 1):
+            if c < X_CHUNKS:
+                x_grouped_tiles.append(transpose_x_chunk(c))
+            if c >= 1:
+                quantise_x_chunk(c - 1, x_grouped_tiles[c - 1])
+
+        def side_by_side(rows, grouped, cols):
+            source = rows[:, :, cols].rearrange("p j (c i) -> p c j i", i=RUN)
+            target = grouped[:, cols, :].rearrange("p (c i) j -> p c j i", i=RUN)
+            return target, source
+
+        def regroup_unit(unit):
+            grouped = grouped_pool.tile([P, UNIT_COLS, PACK], BF16, align_bytes=64)
+            scalar_cols = W1_SCALAR_COLS if unit < W1_UNITS else W2_SCALAR_COLS
+            split = UNIT_COLS - scalar_cols
+            target, source = side_by_side(unit_rows[unit], grouped, slice(0, split))
+            nc.vector.tensor_copy(out=target, in_=source)
+            target, source = side_by_side(unit_rows[unit], grouped, slice(split, UNIT_COLS))
+            nc.scalar.copy(out=target, in_=source)
+            return grouped
+
+        def quantise_unit(grouped):
+            codes = mx_pool.tile([P, UNIT_COLS], U32, align_bytes=64)
+            scales = mx_pool.tile([P, UNIT_COLS], U8, align_bytes=64)
+            nc.vector.quantize_mx(
+                out=codes[:].bitcast(FP8X4),
+                scales=scales[:],
+                in_=grouped[:].rearrange("p n j -> p (n j)"),
+            )
+            return codes, scales
+
+        h_banks = [psum.tile([P, T], F32, tag="bank", name="h%d" % m) for m in range(2 * F_TILES)]
+
+        def first_matmul(s, codes, scales):
+            tokens = slice(s * T, (s + 1) * T)
+            for m in range(2 * F_TILES):
+                w1_cols = slice(m * P, (m + 1) * P)
+                nc.tensor.matmul_mx(
+                    out=h_banks[m][:],
+                    lhsT=codes[:, w1_cols].bitcast(FP8X4),
+                    lhsT_scale=scales[:, w1_cols],
+                    rhs=x_codes[:, tokens].bitcast(FP8X4),
+                    rhs_scale=x_scales[:, tokens],
+                    start=(s == 0),
+                    stop=(s == W1_UNITS - 1),
+                )
+
+        g_codes = consts.tile([P, T], U32, align_bytes=64)
+        g_scales = consts.tile([P, T], U8, align_bytes=64)
+
+        def gate():
+            gelu_a = consts.tile([P, F_TILES, T], F32)
+            g_rows = consts.tile([P, F_TILES, T], BF16)
+            g_grouped = consts.tile([P, T, PACK], BF16, align_bytes=64)
+            for j in range(F_TILES):
+                nc.scalar.activation(
+                    out=gelu_a[:, j, :],
+                    in_=h_banks[j][:],
+                    func=mybir.ActivationFunctionType.Gelu_apprx_tanh,
+                )
+                nc.vector.tensor_tensor(
+                    out=g_rows[:, j, :],
+                    in0=gelu_a[:, j, :],
+                    in1=h_banks[F_TILES + j][:],
+                    op=mybir.AluOpType.mult,
+                )
+            target, source = side_by_side(g_rows, g_grouped, slice(0, T))
+            nc.vector.tensor_copy(out=target, in_=source)
+            nc.vector.quantize_mx(
+                out=g_codes[:].bitcast(FP8X4),
+                scales=g_scales[:],
+                in_=g_grouped[:].rearrange("p t j -> p (t j)"),
+            )
+
+        def second_matmul(v, codes, scales):
+            result = out_pool.tile([P, T_TILES, UNIT_COLS], F32)
+            for tt in range(T_TILES):
+                tokens = slice(tt * P, (tt + 1) * P)
+                for n0 in range(0, UNIT_COLS, N_MOVE):
+                    acc = psum.tile([P, N_MOVE], F32, tag="bank")
+                    nc.tensor.matmul_mx(
+                        out=acc[:],
+                        lhsT=g_codes[:, tokens].bitcast(FP8X4),
+                        lhsT_scale=g_scales[:, tokens],
+                        rhs=codes[:, n0 : n0 + N_MOVE].bitcast(FP8X4),
+                        rhs_scale=scales[:, n0 : n0 + N_MOVE],
+                        start=True,
+                        stop=True,
+                    )
+                    nc.scalar.copy(out=result[:, tt, n0 : n0 + N_MOVE], in_=acc[:])
+            nc.sync.dma_start(
+                out=out_rows[:, :, v * UNIT_COLS : (v + 1) * UNIT_COLS], in_=result[:]
+            )
+
+        grouped_tiles = []
+        mx_tiles = []
+        for i in range(UNITS + 2):
+            if i < UNITS:
+                grouped_tiles.append(regroup_unit(i))
+                next_chunk = i // CHUNK_UNITS + RAW_BUFS
+                if i % CHUNK_UNITS == CHUNK_UNITS - 1 and next_chunk < CHUNKS:
+                    load_chunk(next_chunk)
+            if 1 <= i <= UNITS:
+                mx_tiles.append(quantise_unit(grouped_tiles[i - 1]))
+            if i >= 2:
+                codes, scales = mx_tiles[i - 2]
+                if i - 2 < W1_UNITS:
+                    first_matmul(i - 2, codes, scales)
+                else:
+                    second_matmul(i - 2 - W1_UNITS, codes, scales)
+                if i - 2 == W1_UNITS - 1:
+                    gate()

@@ -51,6 +51,7 @@ def tile_expert_k_kernel(tc, x, weight1, weight2, out):
     w2_rows = weight2.rearrange("(j p) n -> p j n", p=P)
 
     with ExitStack() as ctx:
+        ctx.enter_context(tc.manual_schedule())
         consts = ctx.enter_context(tc.tile_pool(name="consts", bufs=1))
         x_raw_pool = ctx.enter_context(tc.tile_pool(name="x_raw", bufs=X_CHUNKS))
         x_grouped_pool = ctx.enter_context(tc.tile_pool(name="x_grouped", bufs=2))

@@ -30,14 +30,11 @@ UNIT_COLS = 1024
 W1_UNITS = H // K_PASS
 W2_UNITS = H // UNIT_COLS
 UNITS = W1_UNITS + W2_UNITS
-CHUNK_UNITS = 2
-W1_CHUNKS = W1_UNITS // CHUNK_UNITS
-CHUNKS = UNITS // CHUNK_UNITS
-RAW_BUFS = 5
+RAW_BUFS = 13
 
 RUN = 4
 W1_SCALAR_COLS = 512
-W2_SCALAR_COLS = 128
+W2_SCALAR_COLS = 160
 
 N_MOVE = 512
 
@@ -47,48 +44,42 @@ def tile_expert_k_kernel(tc, x, weight1, weight2, out):
 
     x_rows = x.rearrange("e (tt p) h -> p (e tt) h", p=P)
     out_rows = out.rearrange("e (tt p) h -> p (e tt) h", p=P)
-    w1_chunks = weight1.rearrange("(c u p j) n -> c p u (j n)", u=CHUNK_UNITS, p=P, j=PACK)
+    w1_units = weight1.rearrange("(s p j) n -> s p j n", p=P, j=PACK)
     w2_rows = weight2.rearrange("(j p) n -> p j n", p=P)
 
     with ExitStack() as ctx:
         ctx.enter_context(tc.manual_schedule())
         consts = ctx.enter_context(tc.tile_pool(name="consts", bufs=1))
-        x_raw_pool = ctx.enter_context(tc.tile_pool(name="x_raw", bufs=X_CHUNKS))
         x_grouped_pool = ctx.enter_context(tc.tile_pool(name="x_grouped", bufs=2))
         raw_pool = ctx.enter_context(tc.tile_pool(name="raw", bufs=RAW_BUFS))
         grouped_pool = ctx.enter_context(tc.tile_pool(name="grouped", bufs=3))
-        mx_pool = ctx.enter_context(tc.tile_pool(name="mx", bufs=4))
-        out_pool = ctx.enter_context(tc.tile_pool(name="out", bufs=3))
+        mx_pool = ctx.enter_context(tc.tile_pool(name="mx", bufs=5))
+        out_pool = ctx.enter_context(tc.tile_pool(name="out", bufs=6))
         psum = ctx.enter_context(tc.psum_pool(name="psum", bufs=8))
 
         x_raw = []
         for c in range(X_CHUNKS):
-            x_chunk = x_raw_pool.tile([P, T_TILES, X_CHUNK_COLS], BF16)
+            x_chunk = raw_pool.tile([P, T_TILES, X_CHUNK_COLS], BF16, tag="raw")
             cols = slice(c * X_CHUNK_COLS, (c + 1) * X_CHUNK_COLS)
             nc.sync.dma_start(out=x_chunk[:], in_=x_rows[:, :, cols])
             x_raw.append(x_chunk)
 
         unit_rows = []
 
-        def load_chunk(chunk):
-            if chunk < W1_CHUNKS:
-                raw1 = raw_pool.tile([P, CHUNK_UNITS, PACK, UNIT_COLS], BF16, tag="raw")
-                nc.sync.dma_start(
-                    out=raw1[:].rearrange("p u j n -> p u (j n)"), in_=w1_chunks[chunk]
-                )
-                for u in range(CHUNK_UNITS):
-                    unit_rows.append(raw1[:, u])
+        def load_next_unit():
+            unit = len(unit_rows)
+            if unit == UNITS:
+                return
+            rows = raw_pool.tile([P, PACK, UNIT_COLS], BF16, tag="raw")
+            if unit < W1_UNITS:
+                nc.sync.dma_start(out=rows[:], in_=w1_units[unit])
             else:
-                raw2 = raw_pool.tile([P, PACK, CHUNK_UNITS * UNIT_COLS], BF16, tag="raw")
-                first = (chunk - W1_CHUNKS) * CHUNK_UNITS * UNIT_COLS
-                nc.sync.dma_start(
-                    out=raw2[:], in_=w2_rows[:, :, first : first + CHUNK_UNITS * UNIT_COLS]
-                )
-                for u in range(CHUNK_UNITS):
-                    unit_rows.append(raw2[:, :, u * UNIT_COLS : (u + 1) * UNIT_COLS])
+                first = (unit - W1_UNITS) * UNIT_COLS
+                nc.sync.dma_start(out=rows[:], in_=w2_rows[:, :, first : first + UNIT_COLS])
+            unit_rows.append(rows)
 
-        for chunk in range(RAW_BUFS):
-            load_chunk(chunk)
+        for slot in range(RAW_BUFS - X_CHUNKS):
+            load_next_unit()
 
         identity = consts.tile([P, P], F32)
         make_identity(nc, identity[:])
@@ -133,6 +124,7 @@ def tile_expert_k_kernel(tc, x, weight1, weight2, out):
         for c in range(X_CHUNKS + 1):
             if c < X_CHUNKS:
                 x_grouped_tiles.append(transpose_x_chunk(c))
+                load_next_unit()
             if c >= 1:
                 quantise_x_chunk(c - 1, x_grouped_tiles[c - 1])
 
@@ -204,10 +196,10 @@ def tile_expert_k_kernel(tc, x, weight1, weight2, out):
                 in_=g_grouped[:].rearrange("p t j -> p (t j)"),
             )
 
-        def second_matmul(v, codes, scales):
-            result = out_pool.tile([P, T_TILES, UNIT_COLS], F32)
+        def second_matmul(v, codes, scales, vector_helps):
             for tt in range(T_TILES):
                 tokens = slice(tt * P, (tt + 1) * P)
+                result = out_pool.tile([P, UNIT_COLS], F32)
                 for n0 in range(0, UNIT_COLS, N_MOVE):
                     acc = psum.tile([P, N_MOVE], F32, tag="bank")
                     nc.tensor.matmul_mx(
@@ -219,19 +211,20 @@ def tile_expert_k_kernel(tc, x, weight1, weight2, out):
                         start=True,
                         stop=True,
                     )
-                    nc.scalar.copy(out=result[:, tt, n0 : n0 + N_MOVE], in_=acc[:])
-            nc.sync.dma_start(
-                out=out_rows[:, :, v * UNIT_COLS : (v + 1) * UNIT_COLS], in_=result[:]
-            )
+                    if vector_helps and tt == T_TILES - 1:
+                        nc.vector.tensor_copy(out=result[:, n0 : n0 + N_MOVE], in_=acc[:])
+                    else:
+                        nc.scalar.copy(out=result[:, n0 : n0 + N_MOVE], in_=acc[:])
+                nc.sync.dma_start(
+                    out=out_rows[:, tt, v * UNIT_COLS : (v + 1) * UNIT_COLS], in_=result[:]
+                )
 
         grouped_tiles = []
         mx_tiles = []
         for i in range(UNITS + 2):
             if i < UNITS:
                 grouped_tiles.append(regroup_unit(i))
-                next_chunk = i // CHUNK_UNITS + RAW_BUFS
-                if i % CHUNK_UNITS == CHUNK_UNITS - 1 and next_chunk < CHUNKS:
-                    load_chunk(next_chunk)
+                load_next_unit()
             if 1 <= i <= UNITS:
                 mx_tiles.append(quantise_unit(grouped_tiles[i - 1]))
             if i >= 2:
@@ -239,6 +232,6 @@ def tile_expert_k_kernel(tc, x, weight1, weight2, out):
                 if i - 2 < W1_UNITS:
                     first_matmul(i - 2, codes, scales)
                 else:
-                    second_matmul(i - 2 - W1_UNITS, codes, scales)
+                    second_matmul(i - 2 - W1_UNITS, codes, scales, vector_helps=(i >= UNITS))
                 if i - 2 == W1_UNITS - 1:
                     gate()

@@ -17,14 +17,13 @@ T = 256
 H = 8192
 F = 512
 T_TILES = T // P
-F_TILES = F // P
 
 FLOPS = 2 * T * H * (2 * F) + 2 * T * F * H
 
 X_CHUNK_PASSES = 4
 X_CHUNKS = H // (K_PASS * X_CHUNK_PASSES)
 X_CHUNK_COLS = K_PASS * X_CHUNK_PASSES
-WORD_PAIRS = 2
+PAIRS = 2
 
 UNIT_COLS = 1024
 W1_UNITS = H // K_PASS
@@ -33,6 +32,7 @@ UNITS = W1_UNITS + W2_UNITS
 RAW_BUFS = 13
 
 RUN = 4
+EARLY_SCALAR_COLS = 384
 W1_SCALAR_COLS = 512
 W2_SCALAR_COLS = 160
 
@@ -45,7 +45,7 @@ def tile_expert_k_kernel(tc, x, weight1, weight2, out):
     x_rows = x.rearrange("e (tt p) h -> p (e tt) h", p=P)
     out_rows = out.rearrange("e (tt p) h -> p (e tt) h", p=P)
     w1_units = weight1.rearrange("(s p j) n -> s p j n", p=P, j=PACK)
-    w2_rows = weight2.rearrange("(j p) n -> p j n", p=P)
+    w2_rows = weight2.rearrange("(p j) n -> p j n", p=P)
 
     with ExitStack() as ctx:
         ctx.enter_context(tc.manual_schedule())
@@ -55,31 +55,38 @@ def tile_expert_k_kernel(tc, x, weight1, weight2, out):
         grouped_pool = ctx.enter_context(tc.tile_pool(name="grouped", bufs=3))
         mx_pool = ctx.enter_context(tc.tile_pool(name="mx", bufs=5))
         out_pool = ctx.enter_context(tc.tile_pool(name="out", bufs=6))
-        psum = ctx.enter_context(tc.psum_pool(name="psum", bufs=8))
+        h_psum = ctx.enter_context(tc.psum_pool(name="h_psum", bufs=1))
+        psum = ctx.enter_context(tc.psum_pool(name="psum", bufs=4))
 
-        x_raw = []
-        for c in range(X_CHUNKS):
-            x_chunk = raw_pool.tile([P, T_TILES, X_CHUNK_COLS], BF16, tag="raw")
-            cols = slice(c * X_CHUNK_COLS, (c + 1) * X_CHUNK_COLS)
-            nc.sync.dma_start(out=x_chunk[:], in_=x_rows[:, :, cols])
-            x_raw.append(x_chunk)
+        items = []
+        for u in range(UNITS):
+            if u < X_CHUNKS:
+                items.append(("x", u))
+            items.append(("w", u))
+        raw = {}
+        started = []
 
-        unit_rows = []
-
-        def load_next_unit():
-            unit = len(unit_rows)
-            if unit == UNITS:
+        def load_next():
+            n = len(started)
+            if n == len(items):
                 return
-            rows = raw_pool.tile([P, PACK, UNIT_COLS], BF16, tag="raw")
-            if unit < W1_UNITS:
-                nc.sync.dma_start(out=rows[:], in_=w1_units[unit])
+            kind, idx = items[n]
+            if kind == "x":
+                tile = raw_pool.tile([P, T_TILES, X_CHUNK_COLS], BF16, tag="raw")
+                cols = slice(idx * X_CHUNK_COLS, (idx + 1) * X_CHUNK_COLS)
+                nc.sync.dma_start(out=tile[:], in_=x_rows[:, :, cols])
             else:
-                first = (unit - W1_UNITS) * UNIT_COLS
-                nc.sync.dma_start(out=rows[:], in_=w2_rows[:, :, first : first + UNIT_COLS])
-            unit_rows.append(rows)
+                tile = raw_pool.tile([P, PACK, UNIT_COLS], BF16, tag="raw")
+                if idx < W1_UNITS:
+                    nc.sync.dma_start(out=tile[:], in_=w1_units[idx])
+                else:
+                    first = (idx - W1_UNITS) * UNIT_COLS
+                    nc.sync.dma_start(out=tile[:], in_=w2_rows[:, :, first : first + UNIT_COLS])
+            raw[items[n]] = tile
+            started.append(items[n])
 
-        for slot in range(RAW_BUFS - X_CHUNKS):
-            load_next_unit()
+        for slot in range(RAW_BUFS):
+            load_next()
 
         identity = consts.tile([P, P], F32)
         make_identity(nc, identity[:])
@@ -91,117 +98,158 @@ def tile_expert_k_kernel(tc, x, weight1, weight2, out):
 
         x_codes = consts.tile([P, W1_UNITS * T], U32, align_bytes=64)
         x_scales = consts.tile([P, W1_UNITS * T], U8, align_bytes=64)
+        x_grouped_tiles = {}
 
         def transpose_x_chunk(c):
             x_grouped = x_grouped_pool.tile([P, X_CHUNK_PASSES, T, PACK], BF16, align_bytes=64)
             grouped_words = x_grouped[:].bitcast(F32)
-            x_words = x_raw[c][:].bitcast(F32).rearrange(
-                "p tt (s m w) -> p tt s w m", m=P, w=WORD_PAIRS
+            x_words = raw[("x", c)][:].bitcast(F32).rearrange(
+                "p tt (s m w) -> p tt s w m", m=P, w=PAIRS
             )
             for s in range(X_CHUNK_PASSES):
-                bank = psum.tile([P, WORD_PAIRS, T], F32, tag="bank")
-                for w in range(WORD_PAIRS):
+                bank = psum.tile([P, PAIRS, T], F32, tag="bank")
+                for w in range(PAIRS):
                     for tt in range(T_TILES):
                         nc.tensor.transpose(
                             bank[:, w, tt * P : (tt + 1) * P], x_words[:, tt, s, w, :], identity[:]
                         )
-                pairs = bank[:].rearrange("p w t -> p t w")
-                if s % 2 == 0:
-                    nc.scalar.copy(out=grouped_words[:, s], in_=pairs)
-                else:
-                    nc.vector.tensor_copy(out=grouped_words[:, s], in_=pairs)
-            return x_grouped
+                nc.scalar.copy(out=grouped_words[:, s], in_=bank[:].rearrange("p w t -> p t w"))
+            x_grouped_tiles[c] = x_grouped
 
-        def quantise_x_chunk(c, x_grouped):
+        def quantise_x_chunk(c):
             cols = slice(c * X_CHUNK_PASSES * T, (c + 1) * X_CHUNK_PASSES * T)
             nc.vector.quantize_mx(
                 out=x_codes[:, cols].bitcast(FP8X4),
                 scales=x_scales[:, cols],
-                in_=x_grouped[:].rearrange("p s t j -> p (s t j)"),
+                in_=x_grouped_tiles[c][:].rearrange("p s t j -> p (s t j)"),
             )
 
-        x_grouped_tiles = []
-        for c in range(X_CHUNKS + 1):
-            if c < X_CHUNKS:
-                x_grouped_tiles.append(transpose_x_chunk(c))
-                load_next_unit()
-            if c >= 1:
-                quantise_x_chunk(c - 1, x_grouped_tiles[c - 1])
+        grouped_tiles = {}
+        mx_tiles = {}
 
         def side_by_side(rows, grouped, cols):
             source = rows[:, :, cols].rearrange("p j (c i) -> p c j i", i=RUN)
             target = grouped[:, cols, :].rearrange("p (c i) j -> p c j i", i=RUN)
             return target, source
 
-        def regroup_unit(unit):
-            grouped = grouped_pool.tile([P, UNIT_COLS, PACK], BF16, align_bytes=64)
-            scalar_cols = W1_SCALAR_COLS if unit < W1_UNITS else W2_SCALAR_COLS
-            split = UNIT_COLS - scalar_cols
-            target, source = side_by_side(unit_rows[unit], grouped, slice(0, split))
-            nc.vector.tensor_copy(out=target, in_=source)
-            target, source = side_by_side(unit_rows[unit], grouped, slice(split, UNIT_COLS))
-            nc.scalar.copy(out=target, in_=source)
-            return grouped
+        def split_of(unit):
+            if unit < X_CHUNKS:
+                return UNIT_COLS - EARLY_SCALAR_COLS
+            if unit < W1_UNITS:
+                return UNIT_COLS - W1_SCALAR_COLS
+            return UNIT_COLS - W2_SCALAR_COLS
 
-        def quantise_unit(grouped):
+        def start_unit(unit):
+            grouped = grouped_pool.tile([P, UNIT_COLS, PACK], BF16, align_bytes=64)
+            grouped_tiles[unit] = grouped
+
+        def regroup_vector(unit):
+            target, source = side_by_side(
+                raw[("w", unit)], grouped_tiles[unit], slice(0, split_of(unit))
+            )
+            nc.vector.tensor_copy(out=target, in_=source)
+
+        def regroup_scalar(unit):
+            target, source = side_by_side(
+                raw[("w", unit)], grouped_tiles[unit], slice(split_of(unit), UNIT_COLS)
+            )
+            nc.scalar.copy(out=target, in_=source)
+
+        def regroup_unit(unit):
+            start_unit(unit)
+            regroup_vector(unit)
+            regroup_scalar(unit)
+
+        def quantise_unit(unit):
             codes = mx_pool.tile([P, UNIT_COLS], U32, align_bytes=64)
             scales = mx_pool.tile([P, UNIT_COLS], U8, align_bytes=64)
             nc.vector.quantize_mx(
                 out=codes[:].bitcast(FP8X4),
                 scales=scales[:],
-                in_=grouped[:].rearrange("p n j -> p (n j)"),
+                in_=grouped_tiles[unit][:].rearrange("p n j -> p (n j)"),
             )
-            return codes, scales
+            mx_tiles[unit] = (codes, scales)
 
-        h_banks = [psum.tile([P, T], F32, tag="bank", name="h%d" % m) for m in range(2 * F_TILES)]
+        h_banks = [
+            [h_psum.tile([P, N_MOVE], F32, tag="h%d%d" % (tt, half), name="h%d%d" % (tt, half)) for half in range(2)]
+            for tt in range(T_TILES)
+        ]
 
-        def first_matmul(s, codes, scales):
-            tokens = slice(s * T, (s + 1) * T)
-            for m in range(2 * F_TILES):
-                w1_cols = slice(m * P, (m + 1) * P)
-                nc.tensor.matmul_mx(
-                    out=h_banks[m][:],
-                    lhsT=codes[:, w1_cols].bitcast(FP8X4),
-                    lhsT_scale=scales[:, w1_cols],
-                    rhs=x_codes[:, tokens].bitcast(FP8X4),
-                    rhs_scale=x_scales[:, tokens],
-                    start=(s == 0),
-                    stop=(s == W1_UNITS - 1),
-                )
+        def first_matmul(s):
+            codes, scales = mx_tiles[s]
+            for tt in range(T_TILES):
+                tokens = slice(s * T + tt * P, s * T + (tt + 1) * P)
+                for half in range(2):
+                    cols = slice(half * N_MOVE, (half + 1) * N_MOVE)
+                    nc.tensor.matmul_mx(
+                        out=h_banks[tt][half][:],
+                        lhsT=x_codes[:, tokens].bitcast(FP8X4),
+                        lhsT_scale=x_scales[:, tokens],
+                        rhs=codes[:, cols].bitcast(FP8X4),
+                        rhs_scale=scales[:, cols],
+                        start=(s == 0),
+                        stop=(s == W1_UNITS - 1),
+                    )
 
+        gelu_a = consts.tile([P, T_TILES, F], F32)
+        g_rows = consts.tile([P, T_TILES, F], BF16)
+        g_grouped = consts.tile([P, T, PACK], BF16, align_bytes=64)
         g_codes = consts.tile([P, T], U32, align_bytes=64)
         g_scales = consts.tile([P, T], U8, align_bytes=64)
 
-        def gate():
-            gelu_a = consts.tile([P, F_TILES, T], F32)
-            g_rows = consts.tile([P, F_TILES, T], BF16)
-            g_grouped = consts.tile([P, T, PACK], BF16, align_bytes=64)
-            for j in range(F_TILES):
-                nc.scalar.activation(
-                    out=gelu_a[:, j, :],
-                    in_=h_banks[j][:],
-                    func=mybir.ActivationFunctionType.Gelu_apprx_tanh,
-                )
-                nc.vector.tensor_tensor(
-                    out=g_rows[:, j, :],
-                    in0=gelu_a[:, j, :],
-                    in1=h_banks[F_TILES + j][:],
-                    op=mybir.AluOpType.mult,
-                )
-            target, source = side_by_side(g_rows, g_grouped, slice(0, T))
-            nc.vector.tensor_copy(out=target, in_=source)
-            nc.vector.quantize_mx(
-                out=g_codes[:].bitcast(FP8X4),
-                scales=g_scales[:],
-                in_=g_grouped[:].rearrange("p t j -> p (t j)"),
+        def gelu(tt):
+            nc.scalar.activation(
+                out=gelu_a[:, tt, :],
+                in_=h_banks[tt][0][:],
+                func=mybir.ActivationFunctionType.Gelu_apprx_tanh,
             )
 
-        def second_matmul(v, codes, scales, vector_helps):
+        def gate(tt):
+            nc.vector.tensor_tensor(
+                out=g_rows[:, tt, :],
+                in0=gelu_a[:, tt, :],
+                in1=h_banks[tt][1][:],
+                op=mybir.AluOpType.mult,
+            )
+
+        def transpose_g(tt):
+            g_words = g_rows[:, tt, :].bitcast(F32).rearrange("p (m w) -> p w m", w=PAIRS)
+            bank = psum.tile([P, PAIRS, P], F32, tag="bank", name="g_bank")
+            for w in range(PAIRS):
+                nc.tensor.transpose(bank[:, w, :], g_words[:, w, :], identity[:])
+            tokens = slice(tt * P, (tt + 1) * P)
+            nc.scalar.copy(
+                out=g_grouped[:, tokens, :].bitcast(F32), in_=bank[:].rearrange("p w t -> p t w")
+            )
+
+        def quantise_g(tt):
+            tokens = slice(tt * P, (tt + 1) * P)
+            nc.vector.quantize_mx(
+                out=g_codes[:, tokens].bitcast(FP8X4),
+                scales=g_scales[:, tokens],
+                in_=g_grouped[:, tokens, :].rearrange("p t j -> p (t j)"),
+            )
+
+        acc_count = []
+
+        def new_acc():
+            n = len(acc_count)
+            acc_count.append(n)
+            if n % 2 == 0:
+                acc = psum.tile([P, N_MOVE], F32, tag="bank", name="acc")
+            else:
+                which = (n // 2) % 4
+                acc = h_psum.tile([P, N_MOVE], F32, tag="h%d%d" % (which // 2, which % 2), name="acc_h")
+            return acc
+
+        def second_matmul(unit, vector_helps):
+            codes, scales = mx_tiles[unit]
+            v = unit - W1_UNITS
             for tt in range(T_TILES):
                 tokens = slice(tt * P, (tt + 1) * P)
                 result = out_pool.tile([P, UNIT_COLS], F32)
                 for n0 in range(0, UNIT_COLS, N_MOVE):
-                    acc = psum.tile([P, N_MOVE], F32, tag="bank")
+                    acc = new_acc()
                     nc.tensor.matmul_mx(
                         out=acc[:],
                         lhsT=g_codes[:, tokens].bitcast(FP8X4),
@@ -219,19 +267,58 @@ def tile_expert_k_kernel(tc, x, weight1, weight2, out):
                     out=out_rows[:, tt, v * UNIT_COLS : (v + 1) * UNIT_COLS], in_=result[:]
                 )
 
-        grouped_tiles = []
-        mx_tiles = []
-        for i in range(UNITS + 2):
+        def lay_out(item):
+            kind, idx = item
+            if kind == "x":
+                transpose_x_chunk(idx)
+            else:
+                regroup_unit(idx)
+            load_next()
+
+        def quantise(item):
+            kind, idx = item
+            if kind == "x":
+                quantise_x_chunk(idx)
+            else:
+                quantise_unit(idx)
+
+        def multiply(item):
+            kind, idx = item
+            if kind == "w":
+                first_matmul(idx)
+
+        w1_items = items[: X_CHUNKS + W1_UNITS]
+        for n in range(len(w1_items)):
+            lay_out(w1_items[n])
+            if n >= 1:
+                quantise(w1_items[n - 1])
+            if n >= 2:
+                multiply(w1_items[n - 2])
+
+        first_w2 = W1_UNITS
+        quantise_unit(first_w2 - 1)
+        first_matmul(first_w2 - 2)
+        first_matmul(first_w2 - 1)
+        regroup_unit(first_w2)
+        load_next()
+        for tt in range(T_TILES):
+            gelu(tt)
+        for tt in range(T_TILES):
+            gate(tt)
+        start_unit(first_w2 + 1)
+        regroup_scalar(first_w2 + 1)
+        quantise_unit(first_w2)
+        for tt in range(T_TILES):
+            transpose_g(tt)
+        for tt in range(T_TILES):
+            quantise_g(tt)
+        regroup_vector(first_w2 + 1)
+        load_next()
+
+        for i in range(first_w2 + 2, UNITS + 2):
             if i < UNITS:
-                grouped_tiles.append(regroup_unit(i))
-                load_next_unit()
-            if 1 <= i <= UNITS:
-                mx_tiles.append(quantise_unit(grouped_tiles[i - 1]))
-            if i >= 2:
-                codes, scales = mx_tiles[i - 2]
-                if i - 2 < W1_UNITS:
-                    first_matmul(i - 2, codes, scales)
-                else:
-                    second_matmul(i - 2 - W1_UNITS, codes, scales, vector_helps=(i >= UNITS))
-                if i - 2 == W1_UNITS - 1:
-                    gate()
+                regroup_unit(i)
+                load_next()
+            if i - 1 < UNITS:
+                quantise_unit(i - 1)
+            second_matmul(i - 2, vector_helps=(i >= UNITS))

@@ -20,16 +20,19 @@ T_TILES = T // P
 
 FLOPS = 2 * T * H * (2 * F) + 2 * T * F * H
 
-X_CHUNK_PASSES = 4
-X_CHUNKS = H // (K_PASS * X_CHUNK_PASSES)
+X_CHUNK_PASSES = 8
 X_CHUNK_COLS = K_PASS * X_CHUNK_PASSES
+X_CHUNKS = T_TILES * H // X_CHUNK_COLS
+PASSES_PER_BANK = 2
 PAIRS = 2
 
 UNIT_COLS = 1024
 W1_UNITS = H // K_PASS
 W2_UNITS = H // UNIT_COLS
 UNITS = W1_UNITS + W2_UNITS
-RAW_BUFS = 13
+SLOT_BYTES = 8192
+SLOTS = 14
+W2_PAIRS = W2_UNITS // 2
 
 RUN = 4
 EARLY_SCALAR_COLS = 384
@@ -51,7 +54,7 @@ def tile_expert_k_kernel(tc, x, weight1, weight2, out):
         ctx.enter_context(tc.manual_schedule())
         consts = ctx.enter_context(tc.tile_pool(name="consts", bufs=1))
         x_grouped_pool = ctx.enter_context(tc.tile_pool(name="x_grouped", bufs=2))
-        raw_pool = ctx.enter_context(tc.tile_pool(name="raw", bufs=RAW_BUFS))
+        raw_pool = ctx.enter_context(tc.tile_pool(name="raw", bufs=1))
         grouped_pool = ctx.enter_context(tc.tile_pool(name="grouped", bufs=3))
         mx_pool = ctx.enter_context(tc.tile_pool(name="mx", bufs=5))
         out_pool = ctx.enter_context(tc.tile_pool(name="out", bufs=6))
@@ -59,34 +62,51 @@ def tile_expert_k_kernel(tc, x, weight1, weight2, out):
         psum = ctx.enter_context(tc.psum_pool(name="psum", bufs=4))
 
         items = []
-        for u in range(UNITS):
+        for u in range(W1_UNITS):
             if u < X_CHUNKS:
                 items.append(("x", u))
             items.append(("w", u))
         raw = {}
-        started = []
 
-        def load_next():
-            n = len(started)
-            if n == len(items):
-                return
+        def load_item(n):
             kind, idx = items[n]
+            slot = n % SLOTS
             if kind == "x":
-                tile = raw_pool.tile([P, T_TILES, X_CHUNK_COLS], BF16, tag="raw")
-                cols = slice(idx * X_CHUNK_COLS, (idx + 1) * X_CHUNK_COLS)
-                nc.sync.dma_start(out=tile[:], in_=x_rows[:, :, cols])
+                chunk = raw_pool.tile(
+                    [P, X_CHUNK_COLS], BF16, tag="slot%d" % slot, offset=slot * SLOT_BYTES, name="chunk"
+                )
+                first = (idx // T_TILES) * X_CHUNK_COLS
+                nc.sync.dma_start(
+                    out=chunk[:], in_=x_rows[:, idx % T_TILES, first : first + X_CHUNK_COLS]
+                )
+                raw[items[n]] = chunk
             else:
-                tile = raw_pool.tile([P, PACK, UNIT_COLS], BF16, tag="raw")
-                if idx < W1_UNITS:
-                    nc.sync.dma_start(out=tile[:], in_=w1_units[idx])
-                else:
-                    first = (idx - W1_UNITS) * UNIT_COLS
-                    nc.sync.dma_start(out=tile[:], in_=w2_rows[:, :, first : first + UNIT_COLS])
-            raw[items[n]] = tile
-            started.append(items[n])
+                rows = raw_pool.tile(
+                    [P, PACK, UNIT_COLS], BF16, tag="slot%d" % slot, offset=slot * SLOT_BYTES, name="rows"
+                )
+                nc.sync.dma_start(out=rows[:], in_=w1_units[idx])
+                raw[items[n]] = rows[:]
 
-        for slot in range(RAW_BUFS):
-            load_next()
+        def load_pair(m):
+            slot = (len(items) + 2 * m) % SLOTS
+            pair = raw_pool.tile(
+                [P, PACK, 2 * UNIT_COLS], BF16, tag="pair%d" % slot, offset=slot * SLOT_BYTES, name="pair"
+            )
+            first = 2 * m * UNIT_COLS
+            nc.sync.dma_start(out=pair[:], in_=w2_rows[:, :, first : first + 2 * UNIT_COLS])
+            for h in range(2):
+                raw[("w", W1_UNITS + 2 * m + h)] = pair[:, :, h * UNIT_COLS : (h + 1) * UNIT_COLS]
+
+        def load_into_slot_of(n):
+            if n + SLOTS < len(items):
+                load_item(n + SLOTS)
+            else:
+                past = n + SLOTS - len(items)
+                if past % 2 == 1 and past // 2 < W2_PAIRS:
+                    load_pair(past // 2)
+
+        for n in range(SLOTS):
+            load_item(n)
 
         identity = consts.tile([P, P], F32)
         make_identity(nc, identity[:])
@@ -101,23 +121,26 @@ def tile_expert_k_kernel(tc, x, weight1, weight2, out):
         x_grouped_tiles = {}
 
         def transpose_x_chunk(c):
-            x_grouped = x_grouped_pool.tile([P, X_CHUNK_PASSES, T, PACK], BF16, align_bytes=64)
+            x_grouped = x_grouped_pool.tile([P, X_CHUNK_PASSES, P, PACK], BF16, align_bytes=64)
             grouped_words = x_grouped[:].bitcast(F32)
-            x_words = raw[("x", c)][:].bitcast(F32).rearrange(
-                "p tt (s m w) -> p tt s w m", m=P, w=PAIRS
-            )
-            for s in range(X_CHUNK_PASSES):
-                bank = psum.tile([P, PAIRS, T], F32, tag="bank")
-                for w in range(PAIRS):
-                    for tt in range(T_TILES):
-                        nc.tensor.transpose(
-                            bank[:, w, tt * P : (tt + 1) * P], x_words[:, tt, s, w, :], identity[:]
-                        )
-                nc.scalar.copy(out=grouped_words[:, s], in_=bank[:].rearrange("p w t -> p t w"))
+            x_words = raw[("x", c)][:].bitcast(F32).rearrange("p (s m w) -> p s w m", m=P, w=PAIRS)
+            for s0 in range(0, X_CHUNK_PASSES, PASSES_PER_BANK):
+                bank = psum.tile([P, PASSES_PER_BANK, PAIRS, P], F32, tag="bank")
+                for s in range(PASSES_PER_BANK):
+                    for w in range(PAIRS):
+                        nc.tensor.transpose(bank[:, s, w, :], x_words[:, s0 + s, w, :], identity[:])
+                nc.scalar.copy(
+                    out=grouped_words[:, s0 : s0 + PASSES_PER_BANK],
+                    in_=bank[:].rearrange("p s w t -> p s t w"),
+                )
             x_grouped_tiles[c] = x_grouped
 
+        def x_columns(tt, s):
+            return (tt * W1_UNITS + s) * P
+
         def quantise_x_chunk(c):
-            cols = slice(c * X_CHUNK_PASSES * T, (c + 1) * X_CHUNK_PASSES * T)
+            first = x_columns(c % T_TILES, (c // T_TILES) * X_CHUNK_PASSES)
+            cols = slice(first, first + X_CHUNK_PASSES * P)
             nc.vector.quantize_mx(
                 out=x_codes[:, cols].bitcast(FP8X4),
                 scales=x_scales[:, cols],
@@ -178,7 +201,7 @@ def tile_expert_k_kernel(tc, x, weight1, weight2, out):
         def first_matmul(s):
             codes, scales = mx_tiles[s]
             for tt in range(T_TILES):
-                tokens = slice(s * T + tt * P, s * T + (tt + 1) * P)
+                tokens = slice(x_columns(tt, s), x_columns(tt, s) + P)
                 for half in range(2):
                     cols = slice(half * N_MOVE, (half + 1) * N_MOVE)
                     nc.tensor.matmul_mx(
@@ -267,40 +290,38 @@ def tile_expert_k_kernel(tc, x, weight1, weight2, out):
                     out=out_rows[:, tt, v * UNIT_COLS : (v + 1) * UNIT_COLS], in_=result[:]
                 )
 
-        def lay_out(item):
-            kind, idx = item
+        def lay_out(n):
+            kind, idx = items[n]
             if kind == "x":
                 transpose_x_chunk(idx)
             else:
                 regroup_unit(idx)
-            load_next()
+            load_into_slot_of(n)
 
-        def quantise(item):
-            kind, idx = item
+        def quantise(n):
+            kind, idx = items[n]
             if kind == "x":
                 quantise_x_chunk(idx)
             else:
                 quantise_unit(idx)
 
-        def multiply(item):
-            kind, idx = item
+        def multiply(n):
+            kind, idx = items[n]
             if kind == "w":
                 first_matmul(idx)
 
-        w1_items = items[: X_CHUNKS + W1_UNITS]
-        for n in range(len(w1_items)):
-            lay_out(w1_items[n])
+        for n in range(len(items)):
+            lay_out(n)
             if n >= 1:
-                quantise(w1_items[n - 1])
+                quantise(n - 1)
             if n >= 2:
-                multiply(w1_items[n - 2])
+                multiply(n - 2)
 
         first_w2 = W1_UNITS
         quantise_unit(first_w2 - 1)
         first_matmul(first_w2 - 2)
         first_matmul(first_w2 - 1)
         regroup_unit(first_w2)
-        load_next()
         for tt in range(T_TILES):
             gelu(tt)
         for tt in range(T_TILES):
@@ -313,12 +334,10 @@ def tile_expert_k_kernel(tc, x, weight1, weight2, out):
         for tt in range(T_TILES):
             quantise_g(tt)
         regroup_vector(first_w2 + 1)
-        load_next()
 
         for i in range(first_w2 + 2, UNITS + 2):
             if i < UNITS:
                 regroup_unit(i)
-                load_next()
             if i - 1 < UNITS:
                 quantise_unit(i - 1)
             second_matmul(i - 2, vector_helps=(i >= UNITS))

@@ -32,11 +32,13 @@ W2_UNITS = H // UNIT_COLS
 UNITS = W1_UNITS + W2_UNITS
 SLOT_BYTES = 8192
 SLOTS = 14
-W2_PAIRS = W2_UNITS // 2
+W2_SINGLES = 4
+W2_PAIRS = (W2_UNITS - W2_SINGLES) // 2
 
 RUN = 4
 EARLY_SCALAR_COLS = 384
 W1_SCALAR_COLS = 512
+GATE_UNITS = 2
 W2_SCALAR_COLS = 160
 
 N_MOVE = 512
@@ -66,6 +68,9 @@ def tile_expert_k_kernel(tc, x, weight1, weight2, out):
             if u < X_CHUNKS:
                 items.append(("x", u))
             items.append(("w", u))
+        w1_end = len(items)
+        for u in range(W1_UNITS, W1_UNITS + W2_SINGLES):
+            items.append(("w", u))
         raw = {}
 
         def load_item(n):
@@ -84,7 +89,11 @@ def tile_expert_k_kernel(tc, x, weight1, weight2, out):
                 rows = raw_pool.tile(
                     [P, PACK, UNIT_COLS], BF16, tag="slot%d" % slot, offset=slot * SLOT_BYTES, name="rows"
                 )
-                nc.sync.dma_start(out=rows[:], in_=w1_units[idx])
+                if idx < W1_UNITS:
+                    nc.sync.dma_start(out=rows[:], in_=w1_units[idx])
+                else:
+                    first = (idx - W1_UNITS) * UNIT_COLS
+                    nc.sync.dma_start(out=rows[:], in_=w2_rows[:, :, first : first + UNIT_COLS])
                 raw[items[n]] = rows[:]
 
         def load_pair(m):
@@ -92,10 +101,10 @@ def tile_expert_k_kernel(tc, x, weight1, weight2, out):
             pair = raw_pool.tile(
                 [P, PACK, 2 * UNIT_COLS], BF16, tag="pair%d" % slot, offset=slot * SLOT_BYTES, name="pair"
             )
-            first = 2 * m * UNIT_COLS
+            first = (W2_SINGLES + 2 * m) * UNIT_COLS
             nc.sync.dma_start(out=pair[:], in_=w2_rows[:, :, first : first + 2 * UNIT_COLS])
             for h in range(2):
-                raw[("w", W1_UNITS + 2 * m + h)] = pair[:, :, h * UNIT_COLS : (h + 1) * UNIT_COLS]
+                raw[("w", W1_UNITS + W2_SINGLES + 2 * m + h)] = pair[:, :, h * UNIT_COLS : (h + 1) * UNIT_COLS]
 
         def load_into_slot_of(n):
             if n + SLOTS < len(items):
@@ -158,7 +167,7 @@ def tile_expert_k_kernel(tc, x, weight1, weight2, out):
         def split_of(unit):
             if unit < X_CHUNKS:
                 return UNIT_COLS - EARLY_SCALAR_COLS
-            if unit < W1_UNITS:
+            if unit < W1_UNITS + GATE_UNITS:
                 return UNIT_COLS - W1_SCALAR_COLS
             return UNIT_COLS - W2_SCALAR_COLS
 
@@ -166,16 +175,14 @@ def tile_expert_k_kernel(tc, x, weight1, weight2, out):
             grouped = grouped_pool.tile([P, UNIT_COLS, PACK], BF16, align_bytes=64)
             grouped_tiles[unit] = grouped
 
-        def regroup_vector(unit):
-            target, source = side_by_side(
-                raw[("w", unit)], grouped_tiles[unit], slice(0, split_of(unit))
-            )
+        def regroup_vector(unit, first=0, end=UNIT_COLS):
+            cols = slice(first, first + (end - first) * split_of(unit) // UNIT_COLS)
+            target, source = side_by_side(raw[("w", unit)], grouped_tiles[unit], cols)
             nc.vector.tensor_copy(out=target, in_=source)
 
-        def regroup_scalar(unit):
-            target, source = side_by_side(
-                raw[("w", unit)], grouped_tiles[unit], slice(split_of(unit), UNIT_COLS)
-            )
+        def regroup_scalar(unit, first=0, end=UNIT_COLS):
+            cols = slice(first + (end - first) * split_of(unit) // UNIT_COLS, end)
+            target, source = side_by_side(raw[("w", unit)], grouped_tiles[unit], cols)
             nc.scalar.copy(out=target, in_=source)
 
         def regroup_unit(unit):
@@ -183,36 +190,46 @@ def tile_expert_k_kernel(tc, x, weight1, weight2, out):
             regroup_vector(unit)
             regroup_scalar(unit)
 
-        def quantise_unit(unit):
+        def start_codes(unit):
             codes = mx_pool.tile([P, UNIT_COLS], U32, align_bytes=64)
             scales = mx_pool.tile([P, UNIT_COLS], U8, align_bytes=64)
-            nc.vector.quantize_mx(
-                out=codes[:].bitcast(FP8X4),
-                scales=scales[:],
-                in_=grouped_tiles[unit][:].rearrange("p n j -> p (n j)"),
-            )
             mx_tiles[unit] = (codes, scales)
+
+        def quantise_columns(unit, first, end):
+            codes, scales = mx_tiles[unit]
+            nc.vector.quantize_mx(
+                out=codes[:, first:end].bitcast(FP8X4),
+                scales=scales[:, first:end],
+                in_=grouped_tiles[unit][:, first:end, :].rearrange("p n j -> p (n j)"),
+            )
+
+        def quantise_unit(unit):
+            start_codes(unit)
+            quantise_columns(unit, 0, UNIT_COLS)
 
         h_banks = [
             [h_psum.tile([P, N_MOVE], F32, tag="h%d%d" % (tt, half), name="h%d%d" % (tt, half)) for half in range(2)]
             for tt in range(T_TILES)
         ]
 
-        def first_matmul(s):
+        def first_matmul_half(s, half):
             codes, scales = mx_tiles[s]
+            cols = slice(half * N_MOVE, (half + 1) * N_MOVE)
             for tt in range(T_TILES):
                 tokens = slice(x_columns(tt, s), x_columns(tt, s) + P)
-                for half in range(2):
-                    cols = slice(half * N_MOVE, (half + 1) * N_MOVE)
-                    nc.tensor.matmul_mx(
-                        out=h_banks[tt][half][:],
-                        lhsT=x_codes[:, tokens].bitcast(FP8X4),
-                        lhsT_scale=x_scales[:, tokens],
-                        rhs=codes[:, cols].bitcast(FP8X4),
-                        rhs_scale=scales[:, cols],
-                        start=(s == 0),
-                        stop=(s == W1_UNITS - 1),
-                    )
+                nc.tensor.matmul_mx(
+                    out=h_banks[tt][half][:],
+                    lhsT=x_codes[:, tokens].bitcast(FP8X4),
+                    lhsT_scale=x_scales[:, tokens],
+                    rhs=codes[:, cols].bitcast(FP8X4),
+                    rhs_scale=scales[:, cols],
+                    start=(s == 0),
+                    stop=(s == W1_UNITS - 1),
+                )
+
+        def first_matmul(s):
+            for half in range(2):
+                first_matmul_half(s, half)
 
         gelu_a = consts.tile([P, T_TILES, F], F32)
         g_rows = consts.tile([P, T_TILES, F], BF16)
@@ -310,34 +327,46 @@ def tile_expert_k_kernel(tc, x, weight1, weight2, out):
             if kind == "w":
                 first_matmul(idx)
 
-        for n in range(len(items)):
+        last = w1_end - 1
+        for n in range(last):
             lay_out(n)
             if n >= 1:
                 quantise(n - 1)
             if n >= 2:
                 multiply(n - 2)
 
-        first_w2 = W1_UNITS
-        quantise_unit(first_w2 - 1)
-        first_matmul(first_w2 - 2)
-        first_matmul(first_w2 - 1)
-        regroup_unit(first_w2)
+        unit = W1_UNITS - 1
+        quantise(last - 1)
+        start_unit(unit)
+        start_codes(unit)
+        halves = [(half, half * N_MOVE, (half + 1) * N_MOVE) for half in range(2)]
+        for half, first, end in halves:
+            regroup_vector(unit, first, end)
+            regroup_scalar(unit, first, end)
+        load_into_slot_of(last)
+        multiply(last - 2)
+        multiply(last - 1)
+        for half, first, end in halves:
+            quantise_columns(unit, first, end)
+            first_matmul_half(unit, half)
         for tt in range(T_TILES):
             gelu(tt)
+        regroup_unit(W1_UNITS)
         for tt in range(T_TILES):
             gate(tt)
-        start_unit(first_w2 + 1)
-        regroup_scalar(first_w2 + 1)
-        quantise_unit(first_w2)
         for tt in range(T_TILES):
             transpose_g(tt)
+        regroup_unit(W1_UNITS + 1)
+        quantise_unit(W1_UNITS)
         for tt in range(T_TILES):
             quantise_g(tt)
-        regroup_vector(first_w2 + 1)
 
-        for i in range(first_w2 + 2, UNITS + 2):
+        for i in range(W1_UNITS + 2, UNITS + 2):
             if i < UNITS:
-                regroup_unit(i)
+                start_unit(i)
+                regroup_vector(i)
             if i - 1 < UNITS:
                 quantise_unit(i - 1)
             second_matmul(i - 2, vector_helps=(i >= UNITS))
+            if i < UNITS:
+                regroup_scalar(i)

@@ -32,8 +32,8 @@ W2_UNITS = H // UNIT_COLS
 UNITS = W1_UNITS + W2_UNITS
 SLOT_BYTES = 8192
 SLOTS = 14
-W2_SINGLES = 4
-W2_PAIRS = (W2_UNITS - W2_SINGLES) // 2
+W2_LOADS = (2, 2, 2, 2)
+X_BEFORE_UNIT = (1, 2, 5, 6)
 
 RUN = 4
 EARLY_SCALAR_COLS = 384
@@ -64,16 +64,18 @@ def tile_expert_k_kernel(tc, x, weight1, weight2, out):
         psum = ctx.enter_context(tc.psum_pool(name="psum", bufs=4))
 
         items = []
-        for u in range(W1_UNITS):
-            if u < X_CHUNKS:
-                items.append(("x", u))
+        for u in range(UNITS):
+            for c in range(X_CHUNKS):
+                if X_BEFORE_UNIT[c] == u:
+                    items.append(("x", c))
             items.append(("w", u))
-        w1_end = len(items)
-        for u in range(W1_UNITS, W1_UNITS + W2_SINGLES):
-            items.append(("w", u))
+        w1_end = X_CHUNKS + W1_UNITS
+        loads = [(n, 1) for n in range(w1_end)]
+        for count in W2_LOADS:
+            loads.append((sum(c for n, c in loads), count))
         raw = {}
 
-        def load_item(n):
+        def load(n, count):
             kind, idx = items[n]
             slot = n % SLOTS
             if kind == "x":
@@ -85,37 +87,29 @@ def tile_expert_k_kernel(tc, x, weight1, weight2, out):
                     out=chunk[:], in_=x_rows[:, idx % T_TILES, first : first + X_CHUNK_COLS]
                 )
                 raw[items[n]] = chunk
-            else:
-                rows = raw_pool.tile(
-                    [P, PACK, UNIT_COLS], BF16, tag="slot%d" % slot, offset=slot * SLOT_BYTES, name="rows"
-                )
-                if idx < W1_UNITS:
-                    nc.sync.dma_start(out=rows[:], in_=w1_units[idx])
-                else:
-                    first = (idx - W1_UNITS) * UNIT_COLS
-                    nc.sync.dma_start(out=rows[:], in_=w2_rows[:, :, first : first + UNIT_COLS])
-                raw[items[n]] = rows[:]
-
-        def load_pair(m):
-            slot = (len(items) + 2 * m) % SLOTS
-            pair = raw_pool.tile(
-                [P, PACK, 2 * UNIT_COLS], BF16, tag="pair%d" % slot, offset=slot * SLOT_BYTES, name="pair"
+                return
+            rows = raw_pool.tile(
+                [P, PACK, count * UNIT_COLS],
+                BF16,
+                tag="slot%d_%d" % (slot, count),
+                offset=slot * SLOT_BYTES,
+                name="rows",
             )
-            first = (W2_SINGLES + 2 * m) * UNIT_COLS
-            nc.sync.dma_start(out=pair[:], in_=w2_rows[:, :, first : first + 2 * UNIT_COLS])
-            for h in range(2):
-                raw[("w", W1_UNITS + W2_SINGLES + 2 * m + h)] = pair[:, :, h * UNIT_COLS : (h + 1) * UNIT_COLS]
+            if idx < W1_UNITS:
+                nc.sync.dma_start(out=rows[:], in_=w1_units[idx])
+            else:
+                first = (idx - W1_UNITS) * UNIT_COLS
+                nc.sync.dma_start(out=rows[:], in_=w2_rows[:, :, first : first + count * UNIT_COLS])
+            for k in range(count):
+                raw[("w", idx + k)] = rows[:, :, k * UNIT_COLS : (k + 1) * UNIT_COLS]
 
         def load_into_slot_of(n):
-            if n + SLOTS < len(items):
-                load_item(n + SLOTS)
-            else:
-                past = n + SLOTS - len(items)
-                if past % 2 == 1 and past // 2 < W2_PAIRS:
-                    load_pair(past // 2)
+            for first, count in loads:
+                if first + count - 1 == n + SLOTS:
+                    load(first, count)
 
-        for n in range(SLOTS):
-            load_item(n)
+        for n in range(-SLOTS, 0):
+            load_into_slot_of(n)
 
         identity = consts.tile([P, P], F32)
         make_identity(nc, identity[:])
@@ -322,18 +316,23 @@ def tile_expert_k_kernel(tc, x, weight1, weight2, out):
             else:
                 quantise_unit(idx)
 
-        def multiply(n):
-            kind, idx = items[n]
-            if kind == "w":
-                first_matmul(idx)
+        multiplied = []
+
+        def multiply_up_to(n):
+            for kind, idx in items[:n]:
+                if kind == "w" and idx == len(multiplied) and idx < W1_UNITS - 1:
+                    last_chunk = idx // X_CHUNK_PASSES * T_TILES + T_TILES - 1
+                    if items.index(("x", last_chunk)) <= n:
+                        first_matmul(idx)
+                        multiplied.append(idx)
 
         last = w1_end - 1
         for n in range(last):
             lay_out(n)
             if n >= 1:
                 quantise(n - 1)
-            if n >= 2:
-                multiply(n - 2)
+            if n >= 1:
+                multiply_up_to(n - 1)
 
         unit = W1_UNITS - 1
         quantise(last - 1)
@@ -344,8 +343,7 @@ def tile_expert_k_kernel(tc, x, weight1, weight2, out):
             regroup_vector(unit, first, end)
             regroup_scalar(unit, first, end)
         load_into_slot_of(last)
-        multiply(last - 2)
-        multiply(last - 1)
+        multiply_up_to(last)
         for half, first, end in halves:
             quantise_columns(unit, first, end)
             first_matmul_half(unit, half)

@@ -36,10 +36,13 @@ W2_LOADS = (2, 2, 2, 2)
 X_BEFORE_UNIT = (1, 2, 5, 6)
 
 RUN = 4
-EARLY_SCALAR_COLS = 384
-W1_SCALAR_COLS = 512
+EARLY_SCALAR_COLS = 320
+W1_SCALAR_COLS = 416
 GATE_UNITS = 2
-W2_SCALAR_COLS = 160
+GATE_SCALAR_COLS = 384
+W2_SCALAR_COLS = 0
+W1_TENSOR_COLS = 128
+W2_TENSOR_COLS = 256
 
 N_MOVE = 512
 
@@ -113,6 +116,8 @@ def tile_expert_k_kernel(tc, x, weight1, weight2, out):
 
         identity = consts.tile([P, P], F32)
         make_identity(nc, identity[:])
+        identity_bf16 = consts.tile([P, P], BF16)
+        make_identity(nc, identity_bf16[:])
         warm = consts.tile([P, 2], F32)
         nc.vector.memset(warm[:], 0.0)
         nc.scalar.activation(
@@ -158,26 +163,58 @@ def tile_expert_k_kernel(tc, x, weight1, weight2, out):
             target = grouped[:, cols, :].rearrange("p (c i) j -> p c j i", i=RUN)
             return target, source
 
-        def split_of(unit):
+        def shares_of(unit):
             if unit < X_CHUNKS:
-                return UNIT_COLS - EARLY_SCALAR_COLS
-            if unit < W1_UNITS + GATE_UNITS:
-                return UNIT_COLS - W1_SCALAR_COLS
-            return UNIT_COLS - W2_SCALAR_COLS
+                scalar_cols = EARLY_SCALAR_COLS
+            elif unit < W1_UNITS:
+                scalar_cols = W1_SCALAR_COLS
+            elif unit < W1_UNITS + GATE_UNITS:
+                scalar_cols = GATE_SCALAR_COLS
+            else:
+                scalar_cols = W2_SCALAR_COLS
+            tensor_cols = W1_TENSOR_COLS if unit < W1_UNITS else W2_TENSOR_COLS
+            if unit == W1_UNITS - 1:
+                scalar_cols, tensor_cols = UNIT_COLS // 2, 0
+            return UNIT_COLS - scalar_cols - tensor_cols, scalar_cols, tensor_cols
 
         def start_unit(unit):
             grouped = grouped_pool.tile([P, UNIT_COLS, PACK], BF16, align_bytes=64)
             grouped_tiles[unit] = grouped
 
         def regroup_vector(unit, first=0, end=UNIT_COLS):
-            cols = slice(first, first + (end - first) * split_of(unit) // UNIT_COLS)
+            cols = slice(first, first + (end - first) * shares_of(unit)[0] // UNIT_COLS)
             target, source = side_by_side(raw[("w", unit)], grouped_tiles[unit], cols)
             nc.vector.tensor_copy(out=target, in_=source)
 
+        def regroup_tensor(unit, first=0, end=UNIT_COLS):
+            width = (end - first) * shares_of(unit)[2] // UNIT_COLS
+            bank = psum.tile([P, width, PACK], BF16, tag="bank", name="layout")
+            for j in range(0, PACK, 2):
+                nc.tensor.matmul(
+                    out=bank[:, :, j : j + 2].rearrange("p n j -> p j n"),
+                    lhsT=identity_bf16[:],
+                    rhs=raw[("w", unit)][:, j : j + 2, end - width : end],
+                    start=True,
+                    stop=True,
+                )
+            return bank
+
         def regroup_scalar(unit, first=0, end=UNIT_COLS):
-            cols = slice(first + (end - first) * split_of(unit) // UNIT_COLS, end)
-            target, source = side_by_side(raw[("w", unit)], grouped_tiles[unit], cols)
-            nc.scalar.copy(out=target, in_=source)
+            vector_cols, scalar_cols, tensor_cols = shares_of(unit)
+            if tensor_cols:
+                bank = regroup_tensor(unit, first, end)
+            split = first + (end - first) * vector_cols // UNIT_COLS
+            tensor_first = end - (end - first) * tensor_cols // UNIT_COLS
+            if split < tensor_first:
+                target, source = side_by_side(
+                    raw[("w", unit)], grouped_tiles[unit], slice(split, tensor_first)
+                )
+                nc.scalar.copy(out=target, in_=source)
+            if tensor_cols:
+                nc.scalar.copy(
+                    out=grouped_tiles[unit][:, tensor_first:end, :].rearrange("p n j -> p (n j)"),
+                    in_=bank[:].rearrange("p n j -> p (n j)"),
+                )
 
         def regroup_unit(unit):
             start_unit(unit)

@@ -33,6 +33,7 @@ UNITS = W1_UNITS + W2_UNITS
 SLOT_BYTES = 8192
 SLOTS = 14
 W2_LOADS = (2, 2, 2, 2)
+STORES = (2, 2, 1, 1, 1, 1)
 X_BEFORE_UNIT = (1, 2, 5, 6)
 
 RUN = 4
@@ -313,12 +314,30 @@ def tile_expert_k_kernel(tc, x, weight1, weight2, out):
                 acc = h_psum.tile([P, N_MOVE], F32, tag="h%d%d" % (which // 2, which % 2), name="acc_h")
             return acc
 
+        results = {}
+        store_of = []
+        for count in STORES:
+            store_of.extend([(part, count) for part in range(count)])
+
         def second_matmul(unit, vector_helps):
             codes, scales = mx_tiles[unit]
             v = unit - W1_UNITS
+            part, count = store_of[v]
             for tt in range(T_TILES):
                 tokens = slice(tt * P, (tt + 1) * P)
-                result = out_pool.tile([P, UNIT_COLS], F32)
+                if part == 0 and count == 1:
+                    result = out_pool.tile([P, UNIT_COLS], F32)
+                    results[tt] = result
+                elif part == 0:
+                    slot = v + tt
+                    wide = raw_pool.tile(
+                        [P, count * UNIT_COLS],
+                        F32,
+                        tag="out%d" % slot,
+                        offset=slot * SLOT_BYTES,
+                        name="wide",
+                    )
+                    results[tt] = wide
                 for n0 in range(0, UNIT_COLS, N_MOVE):
                     acc = new_acc()
                     nc.tensor.matmul_mx(
@@ -330,13 +349,16 @@ def tile_expert_k_kernel(tc, x, weight1, weight2, out):
                         start=True,
                         stop=True,
                     )
+                    to = results[tt][:, part * UNIT_COLS + n0 : part * UNIT_COLS + n0 + N_MOVE]
                     if vector_helps and tt == T_TILES - 1:
-                        nc.vector.tensor_copy(out=result[:, n0 : n0 + N_MOVE], in_=acc[:])
+                        nc.vector.tensor_copy(out=to, in_=acc[:])
                     else:
-                        nc.scalar.copy(out=result[:, n0 : n0 + N_MOVE], in_=acc[:])
-                nc.sync.dma_start(
-                    out=out_rows[:, tt, v * UNIT_COLS : (v + 1) * UNIT_COLS], in_=result[:]
-                )
+                        nc.scalar.copy(out=to, in_=acc[:])
+                if part == count - 1:
+                    first = (v - part) * UNIT_COLS
+                    nc.sync.dma_start(
+                        out=out_rows[:, tt, first : first + count * UNIT_COLS], in_=results[tt][:]
+                    )
 
         def lay_out(n):
             kind, idx = items[n]

@@ -36,7 +36,7 @@ W2_LOADS = (2, 2, 2, 2)
 STORES = (2, 2, 1, 1, 1, 1)
 X_BEFORE_UNIT = (1, 2, 5, 6)
 
-RUN = 4
+RUN = 2
 EARLY_SCALAR_COLS = 320
 W1_SCALAR_COLS = 416
 GATE_UNITS = 2

from contextlib import ExitStack

import concourse.mybir as mybir
from concourse.masks import make_identity

BF16 = mybir.dt.bfloat16
F32 = mybir.dt.float32
U32 = mybir.dt.uint32
U8 = mybir.dt.uint8
FP8X4 = mybir.dt.float8_e4m3fn_x4

P = 128
PACK = 4
K_PASS = P * PACK

T = 256
H = 8192
F = 512
T_TILES = T // P

FLOPS = 2 * T * H * (2 * F) + 2 * T * F * H

X_CHUNK_PASSES = 8
X_CHUNK_COLS = K_PASS * X_CHUNK_PASSES
X_CHUNKS = T_TILES * H // X_CHUNK_COLS
PASSES_PER_BANK = 2
PAIRS = 2

UNIT_COLS = 1024
W1_UNITS = H // K_PASS
W2_UNITS = H // UNIT_COLS
UNITS = W1_UNITS + W2_UNITS
SLOT_BYTES = 8192
SLOTS = 14
W2_LOADS = (2, 2, 2, 2)
STORES = (2, 2, 1, 1, 1, 1)
X_BEFORE_UNIT = (1, 2, 5, 6)

RUN = 2
EARLY_SCALAR_COLS = 320
W1_SCALAR_COLS = 416
GATE_UNITS = 2
GATE_SCALAR_COLS = 384
W2_SCALAR_COLS = 0
W1_TENSOR_COLS = 128
W2_TENSOR_COLS = 256

N_MOVE = 512


def tile_expert_k_kernel(tc, x, weight1, weight2, out):
    nc = tc.nc

    x_rows = x.rearrange("e (tt p) h -> p (e tt) h", p=P)
    out_rows = out.rearrange("e (tt p) h -> p (e tt) h", p=P)
    w1_units = weight1.rearrange("(s p j) n -> s p j n", p=P, j=PACK)
    w2_rows = weight2.rearrange("(p j) n -> p j n", p=P)

    with ExitStack() as ctx:
        ctx.enter_context(tc.manual_schedule())
        consts = ctx.enter_context(tc.tile_pool(name="consts", bufs=1))
        x_grouped_pool = ctx.enter_context(tc.tile_pool(name="x_grouped", bufs=2))
        raw_pool = ctx.enter_context(tc.tile_pool(name="raw", bufs=1))
        grouped_pool = ctx.enter_context(tc.tile_pool(name="grouped", bufs=3))
        mx_pool = ctx.enter_context(tc.tile_pool(name="mx", bufs=5))
        out_pool = ctx.enter_context(tc.tile_pool(name="out", bufs=6))
        h_psum = ctx.enter_context(tc.psum_pool(name="h_psum", bufs=1))
        psum = ctx.enter_context(tc.psum_pool(name="psum", bufs=4))

        items = []
        for u in range(UNITS):
            for c in range(X_CHUNKS):
                if X_BEFORE_UNIT[c] == u:
                    items.append(("x", c))
            items.append(("w", u))
        w1_end = X_CHUNKS + W1_UNITS
        loads = [(n, 1) for n in range(w1_end)]
        for count in W2_LOADS:
            loads.append((sum(c for n, c in loads), count))
        raw = {}

        def load(n, count):
            kind, idx = items[n]
            slot = n % SLOTS
            if kind == "x":
                chunk = raw_pool.tile(
                    [P, X_CHUNK_COLS], BF16, tag="slot%d" % slot, offset=slot * SLOT_BYTES, name="chunk"
                )
                first = (idx // T_TILES) * X_CHUNK_COLS
                nc.sync.dma_start(
                    out=chunk[:], in_=x_rows[:, idx % T_TILES, first : first + X_CHUNK_COLS]
                )
                raw[items[n]] = chunk
                return
            rows = raw_pool.tile(
                [P, PACK, count * UNIT_COLS],
                BF16,
                tag="slot%d_%d" % (slot, count),
                offset=slot * SLOT_BYTES,
                name="rows",
            )
            if idx < W1_UNITS:
                nc.sync.dma_start(out=rows[:], in_=w1_units[idx])
            else:
                first = (idx - W1_UNITS) * UNIT_COLS
                nc.sync.dma_start(out=rows[:], in_=w2_rows[:, :, first : first + count * UNIT_COLS])
            for k in range(count):
                raw[("w", idx + k)] = rows[:, :, k * UNIT_COLS : (k + 1) * UNIT_COLS]

        def load_into_slot_of(n):
            for first, count in loads:
                if first + count - 1 == n + SLOTS:
                    load(first, count)

        for n in range(-SLOTS, 0):
            load_into_slot_of(n)

        identity = consts.tile([P, P], F32)
        make_identity(nc, identity[:])
        identity_bf16 = consts.tile([P, P], BF16)
        make_identity(nc, identity_bf16[:])
        warm = consts.tile([P, 2], F32)
        nc.vector.memset(warm[:], 0.0)
        nc.scalar.activation(
            out=warm[:, 1:2], in_=warm[:, 0:1], func=mybir.ActivationFunctionType.Gelu_apprx_tanh
        )

        x_codes = consts.tile([P, W1_UNITS * T], U32, align_bytes=64)
        x_scales = consts.tile([P, W1_UNITS * T], U8, align_bytes=64)
        x_grouped_tiles = {}

        def transpose_x_chunk(c):
            x_grouped = x_grouped_pool.tile([P, X_CHUNK_PASSES, P, PACK], BF16, align_bytes=64)
            grouped_words = x_grouped[:].bitcast(F32)
            x_words = raw[("x", c)][:].bitcast(F32).rearrange("p (s m w) -> p s w m", m=P, w=PAIRS)
            for s0 in range(0, X_CHUNK_PASSES, PASSES_PER_BANK):
                bank = psum.tile([P, PASSES_PER_BANK, PAIRS, P], F32, tag="bank")
                for s in range(PASSES_PER_BANK):
                    for w in range(PAIRS):
                        nc.tensor.transpose(bank[:, s, w, :], x_words[:, s0 + s, w, :], identity[:])
                nc.scalar.copy(
                    out=grouped_words[:, s0 : s0 + PASSES_PER_BANK],
                    in_=bank[:].rearrange("p s w t -> p s t w"),
                )
            x_grouped_tiles[c] = x_grouped

        def x_columns(tt, s):
            return (tt * W1_UNITS + s) * P

        def quantise_x_chunk(c):
            first = x_columns(c % T_TILES, (c // T_TILES) * X_CHUNK_PASSES)
            cols = slice(first, first + X_CHUNK_PASSES * P)
            nc.vector.quantize_mx(
                out=x_codes[:, cols].bitcast(FP8X4),
                scales=x_scales[:, cols],
                in_=x_grouped_tiles[c][:].rearrange("p s t j -> p (s t j)"),
            )

        grouped_tiles = {}
        mx_tiles = {}

        def side_by_side(rows, grouped, cols):
            source = rows[:, :, cols].rearrange("p j (c i) -> p c j i", i=RUN)
            target = grouped[:, cols, :].rearrange("p (c i) j -> p c j i", i=RUN)
            return target, source

        def shares_of(unit):
            if unit < X_CHUNKS:
                scalar_cols = EARLY_SCALAR_COLS
            elif unit < W1_UNITS:
                scalar_cols = W1_SCALAR_COLS
            elif unit < W1_UNITS + GATE_UNITS:
                scalar_cols = GATE_SCALAR_COLS
            else:
                scalar_cols = W2_SCALAR_COLS
            tensor_cols = W1_TENSOR_COLS if unit < W1_UNITS else W2_TENSOR_COLS
            if unit == W1_UNITS - 1:
                scalar_cols, tensor_cols = UNIT_COLS // 2, 0
            return UNIT_COLS - scalar_cols - tensor_cols, scalar_cols, tensor_cols

        def start_unit(unit):
            grouped = grouped_pool.tile([P, UNIT_COLS, PACK], BF16, align_bytes=64)
            grouped_tiles[unit] = grouped

        def regroup_vector(unit, first=0, end=UNIT_COLS):
            cols = slice(first, first + (end - first) * shares_of(unit)[0] // UNIT_COLS)
            target, source = side_by_side(raw[("w", unit)], grouped_tiles[unit], cols)
            nc.vector.tensor_copy(out=target, in_=source)

        def regroup_tensor(unit, first=0, end=UNIT_COLS):
            width = (end - first) * shares_of(unit)[2] // UNIT_COLS
            bank = psum.tile([P, width, PACK], BF16, tag="bank", name="layout")
            for j in range(0, PACK, 2):
                nc.tensor.matmul(
                    out=bank[:, :, j : j + 2].rearrange("p n j -> p j n"),
                    lhsT=identity_bf16[:],
                    rhs=raw[("w", unit)][:, j : j + 2, end - width : end],
                    start=True,
                    stop=True,
                )
            return bank

        def regroup_scalar(unit, first=0, end=UNIT_COLS):
            vector_cols, scalar_cols, tensor_cols = shares_of(unit)
            if tensor_cols:
                bank = regroup_tensor(unit, first, end)
            split = first + (end - first) * vector_cols // UNIT_COLS
            tensor_first = end - (end - first) * tensor_cols // UNIT_COLS
            if split < tensor_first:
                target, source = side_by_side(
                    raw[("w", unit)], grouped_tiles[unit], slice(split, tensor_first)
                )
                nc.scalar.copy(out=target, in_=source)
            if tensor_cols:
                nc.scalar.copy(
                    out=grouped_tiles[unit][:, tensor_first:end, :].rearrange("p n j -> p (n j)"),
                    in_=bank[:].rearrange("p n j -> p (n j)"),
                )

        def regroup_unit(unit):
            start_unit(unit)
            regroup_vector(unit)
            regroup_scalar(unit)

        def start_codes(unit):
            codes = mx_pool.tile([P, UNIT_COLS], U32, align_bytes=64)
            scales = mx_pool.tile([P, UNIT_COLS], U8, align_bytes=64)
            mx_tiles[unit] = (codes, scales)

        def quantise_columns(unit, first, end):
            codes, scales = mx_tiles[unit]
            nc.vector.quantize_mx(
                out=codes[:, first:end].bitcast(FP8X4),
                scales=scales[:, first:end],
                in_=grouped_tiles[unit][:, first:end, :].rearrange("p n j -> p (n j)"),
            )

        def quantise_unit(unit):
            start_codes(unit)
            quantise_columns(unit, 0, UNIT_COLS)

        h_banks = [
            [h_psum.tile([P, N_MOVE], F32, tag="h%d%d" % (tt, half), name="h%d%d" % (tt, half)) for half in range(2)]
            for tt in range(T_TILES)
        ]

        def first_matmul_half(s, half):
            codes, scales = mx_tiles[s]
            cols = slice(half * N_MOVE, (half + 1) * N_MOVE)
            for tt in range(T_TILES):
                tokens = slice(x_columns(tt, s), x_columns(tt, s) + P)
                nc.tensor.matmul_mx(
                    out=h_banks[tt][half][:],
                    lhsT=x_codes[:, tokens].bitcast(FP8X4),
                    lhsT_scale=x_scales[:, tokens],
                    rhs=codes[:, cols].bitcast(FP8X4),
                    rhs_scale=scales[:, cols],
                    start=(s == 0),
                    stop=(s == W1_UNITS - 1),
                )

        def first_matmul(s):
            for half in range(2):
                first_matmul_half(s, half)

        gelu_a = consts.tile([P, T_TILES, F], F32)
        g_rows = consts.tile([P, T_TILES, F], BF16)
        g_grouped = consts.tile([P, T, PACK], BF16, align_bytes=64)
        g_codes = consts.tile([P, T], U32, align_bytes=64)
        g_scales = consts.tile([P, T], U8, align_bytes=64)

        def gelu(tt):
            nc.scalar.activation(
                out=gelu_a[:, tt, :],
                in_=h_banks[tt][0][:],
                func=mybir.ActivationFunctionType.Gelu_apprx_tanh,
            )

        def gate(tt):
            nc.vector.tensor_tensor(
                out=g_rows[:, tt, :],
                in0=gelu_a[:, tt, :],
                in1=h_banks[tt][1][:],
                op=mybir.AluOpType.mult,
            )

        def transpose_g(tt):
            g_words = g_rows[:, tt, :].bitcast(F32).rearrange("p (m w) -> p w m", w=PAIRS)
            bank = psum.tile([P, PAIRS, P], F32, tag="bank", name="g_bank")
            for w in range(PAIRS):
                nc.tensor.transpose(bank[:, w, :], g_words[:, w, :], identity[:])
            tokens = slice(tt * P, (tt + 1) * P)
            nc.scalar.copy(
                out=g_grouped[:, tokens, :].bitcast(F32), in_=bank[:].rearrange("p w t -> p t w")
            )

        def quantise_g(tt):
            tokens = slice(tt * P, (tt + 1) * P)
            nc.vector.quantize_mx(
                out=g_codes[:, tokens].bitcast(FP8X4),
                scales=g_scales[:, tokens],
                in_=g_grouped[:, tokens, :].rearrange("p t j -> p (t j)"),
            )

        acc_count = []

        def new_acc():
            n = len(acc_count)
            acc_count.append(n)
            if n % 2 == 0:
                acc = psum.tile([P, N_MOVE], F32, tag="bank", name="acc")
            else:
                which = (n // 2) % 4
                acc = h_psum.tile([P, N_MOVE], F32, tag="h%d%d" % (which // 2, which % 2), name="acc_h")
            return acc

        results = {}
        store_of = []
        for count in STORES:
            store_of.extend([(part, count) for part in range(count)])

        def second_matmul(unit, vector_helps):
            codes, scales = mx_tiles[unit]
            v = unit - W1_UNITS
            part, count = store_of[v]
            for tt in range(T_TILES):
                tokens = slice(tt * P, (tt + 1) * P)
                if part == 0 and count == 1:
                    result = out_pool.tile([P, UNIT_COLS], F32)
                    results[tt] = result
                elif part == 0:
                    slot = v + tt
                    wide = raw_pool.tile(
                        [P, count * UNIT_COLS],
                        F32,
                        tag="out%d" % slot,
                        offset=slot * SLOT_BYTES,
                        name="wide",
                    )
                    results[tt] = wide
                for n0 in range(0, UNIT_COLS, N_MOVE):
                    acc = new_acc()
                    nc.tensor.matmul_mx(
                        out=acc[:],
                        lhsT=g_codes[:, tokens].bitcast(FP8X4),
                        lhsT_scale=g_scales[:, tokens],
                        rhs=codes[:, n0 : n0 + N_MOVE].bitcast(FP8X4),
                        rhs_scale=scales[:, n0 : n0 + N_MOVE],
                        start=True,
                        stop=True,
                    )
                    to = results[tt][:, part * UNIT_COLS + n0 : part * UNIT_COLS + n0 + N_MOVE]
                    if vector_helps and tt == T_TILES - 1:
                        nc.vector.tensor_copy(out=to, in_=acc[:])
                    else:
                        nc.scalar.copy(out=to, in_=acc[:])
                if part == count - 1:
                    first = (v - part) * UNIT_COLS
                    nc.sync.dma_start(
                        out=out_rows[:, tt, first : first + count * UNIT_COLS], in_=results[tt][:]
                    )

        def lay_out(n):
            kind, idx = items[n]
            if kind == "x":
                transpose_x_chunk(idx)
            else:
                regroup_unit(idx)
            load_into_slot_of(n)

        def quantise(n):
            kind, idx = items[n]
            if kind == "x":
                quantise_x_chunk(idx)
            else:
                quantise_unit(idx)

        multiplied = []

        def multiply_up_to(n):
            for kind, idx in items[:n]:
                if kind == "w" and idx == len(multiplied) and idx < W1_UNITS - 1:
                    last_chunk = idx // X_CHUNK_PASSES * T_TILES + T_TILES - 1
                    if items.index(("x", last_chunk)) <= n:
                        first_matmul(idx)
                        multiplied.append(idx)

        last = w1_end - 1
        for n in range(last):
            lay_out(n)
            if n >= 1:
                quantise(n - 1)
            if n >= 1:
                multiply_up_to(n - 1)

        unit = W1_UNITS - 1
        quantise(last - 1)
        start_unit(unit)
        start_codes(unit)
        halves = [(half, half * N_MOVE, (half + 1) * N_MOVE) for half in range(2)]
        for half, first, end in halves:
            regroup_vector(unit, first, end)
            regroup_scalar(unit, first, end)
        load_into_slot_of(last)
        multiply_up_to(last)
        for half, first, end in halves:
            quantise_columns(unit, first, end)
            first_matmul_half(unit, half)
        for tt in range(T_TILES):
            gelu(tt)
        regroup_unit(W1_UNITS)
        for tt in range(T_TILES):
            gate(tt)
        for tt in range(T_TILES):
            transpose_g(tt)
        regroup_unit(W1_UNITS + 1)
        quantise_unit(W1_UNITS)
        for tt in range(T_TILES):
            quantise_g(tt)

        for i in range(W1_UNITS + 2, UNITS + 2):
            if i < UNITS:
                start_unit(i)
                regroup_vector(i)
            if i - 1 < UNITS:
                quantise_unit(i - 1)
            second_matmul(i - 2, vector_helps=(i >= UNITS))
            if i < UNITS:
                regroup_scalar(i)
